import numpy as np
import ml_dtypes


def mxq(x, axis, fmt="e4m3"):
    dtype, down = {"e4m3": (ml_dtypes.float8_e4m3fn, 7), "e5m2": (ml_dtypes.float8_e5m2, 14)}[fmt]
    v = np.moveaxis(np.asarray(x, np.float32).astype(ml_dtypes.bfloat16).astype(np.float64), axis, -1)
    blocks = v.reshape(v.shape[:-1] + (-1, 32))
    amax = np.abs(blocks).max(-1, keepdims=True)
    byte = np.maximum(np.where(amax > 0, np.frexp(amax)[1] - 1 + 127, 0) - down, 1)
    scale = np.exp2(byte - 127.0)
    codes = (blocks / scale).astype(np.float32).astype(dtype).astype(np.float64)
    return np.moveaxis((codes * scale).reshape(v.shape), -1, axis)


WIDE = False


def mx_kscale(k):
    if not WIDE:
        return np.ones(k)
    levels = np.array([10, -10, 5, -5, 0])
    a = np.random.permutation(np.resize(levels, k // 512 * 4)).reshape(k // 512, 4)
    idx = np.arange(k)
    return np.exp2(a[idx // 512, idx % 128 // 32])


BF16 = ml_dtypes.bfloat16


def bf(x):
    return np.asarray(x, np.float32).astype(BF16)


def f64(x):
    return np.asarray(x).astype(np.float64)


B, C, W, H = 8, 512, 16, 32


def setup_inputs():
    t = mx_kscale(C)
    return {"x1": bf(np.random.standard_normal((B, W, H, C)) * t),
            "x2": bf(np.random.standard_normal((B, W, H, C)) * t),
            "x3": bf(np.random.standard_normal((B, W, H, C)) * t),
            "hat": bf(np.random.standard_normal((B, 3 * C))),
            "w2": bf(np.random.standard_normal((C, C)) / np.sqrt(C) / t[None, :]),
            "b2": bf(np.random.standard_normal(C) * 0.1)}


def reference(x1, x2, x3, hat, w2, b2):
    hs = f64(hat).reshape(-1, 3, C)
    e = np.exp(hs - hs.max(axis=1, keepdims=True))
    bar = e / e.sum(axis=1, keepdims=True)
    g = bar[:, :, None, None, :]
    out = g[:, 0] * f64(x1) + g[:, 1] * f64(x2) + g[:, 2] * f64(x3)
    z = (mxq(out, 3, "e4m3") @ mxq(f64(w2), 1, "e4m3").T) + f64(b2)
    return z.transpose(0, 3, 1, 2)

@@ -1,0 +1,184 @@
+from contextlib import ExitStack
+
+import concourse.mybir as mybir
+from concourse.masks import make_identity
+
+F32 = mybir.dt.float32
+BF16 = mybir.dt.bfloat16
+U32 = mybir.dt.uint32
+U8 = mybir.dt.uint8
+FP8X4 = mybir.dt.float8_e4m3fn_x4
+ALU = mybir.AluOpType
+ACT = mybir.ActivationFunctionType
+AX = mybir.AxisListType
+
+P = 128
+B = 8
+C = 512
+TOK = 512
+FLOPS = 2 * B * TOK * C * C
+
+
+def tile_modelnew_pb_t_kernel(tc, x1, x2, x3, hat, w2, b2, out):
+    nc = tc.nc
+    xs = [x1, x2, x3]
+    with ExitStack() as ctx:
+        const = ctx.enter_context(tc.tile_pool(name="const", bufs=1))
+        xin = ctx.enter_context(tc.tile_pool(name="xin", bufs=B))
+        work = ctx.enter_context(tc.tile_pool(name="work", bufs=4))
+        stage = ctx.enter_context(tc.tile_pool(name="stage", bufs=3))
+        psum = ctx.enter_context(tc.psum_pool(name="psum", bufs=2))
+
+        hat_sb = const.tile([P, C], BF16)
+        hat_rows = hat.rearrange("b (k c) -> (b k) c", k=3)
+        nc.sync.dma_start(out=hat_sb[0:24, :], in_=hat_rows)
+        nc.scalar.dma_start(out=hat_sb[24:32, :], in_=hat_rows[0:8, :])
+        nc.vector.memset(hat_sb[32:64, :], 0.0)
+        nc.vector.memset(hat_sb[64:128, :], 0.0)
+        b2_bf = const.tile([P, 4], BF16)
+        nc.scalar.dma_start(out=b2_bf[:], in_=b2.rearrange("(i j) -> i j", j=4))
+
+        warm_in = const.tile([P, 1], F32)
+        warm_out = const.tile([P, 1], F32)
+        nc.vector.memset(warm_in[:], 0.0)
+        nc.scalar.activation(out=warm_out[:], in_=warm_in[:], func=ACT.Exp)
+
+        ident = const.tile([P, P], F32)
+        make_identity(nc, ident[:])
+
+        w_sb = const.tile([P, 4, C], BF16)
+        x_sb = []
+        for b in range(B):
+            row = []
+            for k in range(3):
+                xt = xin.tile([P, 4, C], BF16, name="x%d_%d" % (k, b), tag="x%d" % k)
+                src = xs[k][b].rearrange("w h c -> (w h) c").rearrange("(p j) c -> p j c", j=4)
+                nc.sync.dma_start(out=xt[:], in_=src)
+                row.append(xt)
+            x_sb.append(row)
+            if b == 0:
+                nc.sync.dma_start(out=w_sb[:], in_=w2.rearrange("(i j) c -> i j c", j=4))
+
+        aux_ps = psum.tile([P, 2, P], F32, tag="o")
+        hat_w = hat_sb[:].bitcast(F32)
+        for u in range(2):
+            nc.tensor.transpose(aux_ps[:, u, :], hat_w[:, P * u : P * u + P], ident[:])
+        logit = const.tile([P, 16, 3, 2], F32)
+        nc.vector.tensor_copy(
+            out=logit[:].rearrange("q (u b) k e -> q u (b k e)", u=2),
+            in_=aux_ps[:].bitcast(BF16)[:, :, 0:48],
+        )
+        top = const.tile([P, 16, 2], F32)
+        nc.vector.tensor_reduce(
+            out=top[:], in_=logit[:].rearrange("q a k e -> q a e k"), axis=AX.X, op=ALU.max
+        )
+        shifted = const.tile([P, 16, 3, 2], F32)
+        nc.vector.tensor_tensor(
+            out=shifted[:], in0=logit[:], in1=top[:].unsqueeze(2).to_broadcast([P, 16, 3, 2]),
+            op=ALU.subtract,
+        )
+        expd = const.tile([P, 16, 3, 2], F32)
+        nc.scalar.activation(out=expd[:], in_=shifted[:], func=ACT.Exp)
+        total = const.tile([P, 16, 2], F32)
+        nc.vector.tensor_reduce(
+            out=total[:], in_=expd[:].rearrange("q a k e -> q a e k"), axis=AX.X, op=ALU.add
+        )
+        inv = const.tile([P, 16, 2], F32)
+        nc.vector.reciprocal(out=inv[:], in_=total[:])
+        gate = const.tile([P, 16, 3, 2], F32)
+        nc.vector.tensor_tensor(
+            out=gate[:], in0=expd[:], in1=inv[:].unsqueeze(2).to_broadcast([P, 16, 3, 2]),
+            op=ALU.mult,
+        )
+        b2_f = const.tile([P, 4], F32)
+        nc.vector.tensor_copy(out=b2_f[:], in_=b2_bf[:])
+
+        w_codes = const.tile([P, C], U32, align_bytes=64)
+        w_scales = const.tile([P, C], U8, align_bytes=64)
+
+        def prepare_w():
+            w_words = w_sb[:].bitcast(F32)
+            w_grouped = const.tile([P, 4 * C], BF16, align_bytes=64)
+            w_pairs = w_grouped[:].bitcast(F32).rearrange("q (c u) -> q c u", u=2)
+            for h in range(2):
+                w_ps = psum.tile([P, 2, 2, P], F32, tag="o")
+                for u in range(2):
+                    for jj in range(2):
+                        nc.tensor.transpose(
+                            w_ps[:, u, jj, :], w_words[:, 2 * h + jj, P * u : P * u + P], ident[:]
+                        )
+                nc.vector.tensor_copy(
+                    out=w_pairs[:, 256 * h : 256 * h + 256, :],
+                    in_=w_ps[:].rearrange("q u jj i -> q (jj i) u"),
+                )
+            nc.vector.quantize_mx(out=w_codes[:].bitcast(FP8X4), scales=w_scales[:], in_=w_grouped[:])
+
+        def half_view(bank, e):
+            v = bank[:].bitcast(BF16).rearrange("q j (p e) -> q j p e", e=2)
+            return v[:, :, :, e].rearrange("q j p -> q p j")
+
+        for b in range(B):
+            planes = stage.tile([P, 4, TOK], BF16)
+            for u in range(2):
+                banks = []
+                for k in range(3):
+                    bank = psum.tile([P, 4, P], F32, name="bank%d" % k, tag="t%d" % k)
+                    xw = x_sb[b][k][:].bitcast(F32)
+                    for j in range(4):
+                        nc.tensor.transpose(bank[:, j, :], xw[:, j, P * u : P * u + P], ident[:])
+                    banks.append(bank)
+                a = 8 * u + b
+                t0s = []
+                for e in range(2):
+                    t0 = work.tile([P, P, 4], F32, name="t0")
+                    nc.scalar.activation(
+                        out=t0[:], in_=half_view(banks[0], e), func=ACT.Copy,
+                        scale=gate[:, a, 0, e : e + 1],
+                    )
+                    t0s.append(t0)
+                t1s = []
+                for e in range(2):
+                    t1 = work.tile([P, P, 4], F32, name="t1")
+                    nc.vector.scalar_tensor_tensor(
+                        out=t1[:], in0=half_view(banks[1], e), scalar=gate[:, a, 1, e : e + 1],
+                        in1=t0s[e][:], op0=ALU.mult, op1=ALU.add,
+                    )
+                    t1s.append(t1)
+                for e in range(2):
+                    nc.vector.scalar_tensor_tensor(
+                        out=planes[:, 2 * u + e, :].rearrange("q (p j) -> q p j", j=4),
+                        in0=half_view(banks[2], e), scalar=gate[:, a, 2, e : e + 1],
+                        in1=t1s[e][:], op0=ALU.mult, op1=ALU.add,
+                    )
+            if b == 0:
+                prepare_w()
+            grouped = stage.tile([P, TOK, 4], BF16, align_bytes=64)
+            nc.gpsimd.tensor_scalar(
+                out=grouped[:], in0=planes[:].rearrange("q t n -> q n t"),
+                scalar1=1.0, scalar2=0.0, op0=ALU.mult, op1=ALU.add,
+            )
+            codes = stage.tile([P, TOK], U32, align_bytes=64)
+            scales = stage.tile([P, TOK], U8, align_bytes=64)
+            nc.vector.quantize_mx(
+                out=codes[:].bitcast(FP8X4), scales=scales[:],
+                in_=grouped[:].rearrange("q n t -> q (n t)"),
+            )
+            o_sb = stage.tile([P, 4, TOK], F32)
+            for j in range(4):
+                acc = psum.tile([P, TOK], F32, tag="o")
+                nc.tensor.matmul_mx(
+                    out=acc[:],
+                    lhsT=w_codes[:, P * j : P * j + P].bitcast(FP8X4),
+                    lhsT_scale=w_scales[:, P * j : P * j + P],
+                    rhs=codes[:].bitcast(FP8X4),
+                    rhs_scale=scales[:],
+                    start=True,
+                    stop=True,
+                )
+                nc.scalar.activation(
+                    out=o_sb[:, j, :], in_=acc[:], func=ACT.Identity, bias=b2_f[:, j : j + 1], scale=1.0
+                )
+            nc.scalar.dma_start(
+                out=out[b].rearrange("(i j) w h -> i (j w h)", j=4),
+                in_=o_sb[:].rearrange("i j n -> i (j n)"),
+            )

@@ -16,6 +16,7 @@ P = 128
 B = 8
 C = 512
 TOK = 512
+UNITS = 2 * B
 FLOPS = 2 * B * TOK * C * C
 
 
@@ -28,6 +29,7 @@ def tile_modelnew_pb_t_kernel(tc, x1, x2, x3, hat, w2, b2, out):
         work = ctx.enter_context(tc.tile_pool(name="work", bufs=4))
         stage = ctx.enter_context(tc.tile_pool(name="stage", bufs=3))
         psum = ctx.enter_context(tc.psum_pool(name="psum", bufs=2))
+        ctx.enter_context(tc.manual_schedule())
 
         hat_sb = const.tile([P, C], BF16)
         hat_rows = hat.rearrange("b (k c) -> (b k) c", k=3)
@@ -56,7 +58,7 @@ def tile_modelnew_pb_t_kernel(tc, x1, x2, x3, hat, w2, b2, out):
                 nc.sync.dma_start(out=xt[:], in_=src)
                 row.append(xt)
             x_sb.append(row)
-            if b == 0:
+            if b == 1:
                 nc.sync.dma_start(out=w_sb[:], in_=w2.rearrange("(i j) c -> i j c", j=4))
 
         aux_ps = psum.tile([P, 2, P], F32, tag="o")
@@ -95,10 +97,10 @@ def tile_modelnew_pb_t_kernel(tc, x1, x2, x3, hat, w2, b2, out):
 
         w_codes = const.tile([P, C], U32, align_bytes=64)
         w_scales = const.tile([P, C], U8, align_bytes=64)
+        w_grouped = const.tile([P, 4 * C], BF16, align_bytes=64)
 
-        def prepare_w():
+        def transpose_w():
             w_words = w_sb[:].bitcast(F32)
-            w_grouped = const.tile([P, 4 * C], BF16, align_bytes=64)
             w_pairs = w_grouped[:].bitcast(F32).rearrange("q (c u) -> q c u", u=2)
             for h in range(2):
                 w_ps = psum.tile([P, 2, 2, P], F32, tag="o")
@@ -107,78 +109,140 @@ def tile_modelnew_pb_t_kernel(tc, x1, x2, x3, hat, w2, b2, out):
                         nc.tensor.transpose(
                             w_ps[:, u, jj, :], w_words[:, 2 * h + jj, P * u : P * u + P], ident[:]
                         )
-                nc.vector.tensor_copy(
+                nc.scalar.copy(
                     out=w_pairs[:, 256 * h : 256 * h + 256, :],
                     in_=w_ps[:].rearrange("q u jj i -> q (jj i) u"),
                 )
-            nc.vector.quantize_mx(out=w_codes[:].bitcast(FP8X4), scales=w_scales[:], in_=w_grouped[:])
 
         def half_view(bank, e):
             v = bank[:].bitcast(BF16).rearrange("q j (p e) -> q j p e", e=2)
             return v[:, :, :, e].rearrange("q j p -> q p j")
 
-        for b in range(B):
-            planes = stage.tile([P, 4, TOK], BF16)
-            for u in range(2):
-                banks = []
-                for k in range(3):
-                    bank = psum.tile([P, 4, P], F32, name="bank%d" % k, tag="t%d" % k)
-                    xw = x_sb[b][k][:].bitcast(F32)
-                    for j in range(4):
-                        nc.tensor.transpose(bank[:, j, :], xw[:, j, P * u : P * u + P], ident[:])
-                    banks.append(bank)
-                a = 8 * u + b
-                t0s = []
-                for e in range(2):
-                    t0 = work.tile([P, P, 4], F32, name="t0")
-                    nc.scalar.activation(
-                        out=t0[:], in_=half_view(banks[0], e), func=ACT.Copy,
-                        scale=gate[:, a, 0, e : e + 1],
-                    )
-                    t0s.append(t0)
-                t1s = []
-                for e in range(2):
-                    t1 = work.tile([P, P, 4], F32, name="t1")
-                    nc.vector.scalar_tensor_tensor(
-                        out=t1[:], in0=half_view(banks[1], e), scalar=gate[:, a, 1, e : e + 1],
-                        in1=t0s[e][:], op0=ALU.mult, op1=ALU.add,
-                    )
-                    t1s.append(t1)
-                for e in range(2):
-                    nc.vector.scalar_tensor_tensor(
-                        out=planes[:, 2 * u + e, :].rearrange("q (p j) -> q p j", j=4),
-                        in0=half_view(banks[2], e), scalar=gate[:, a, 2, e : e + 1],
-                        in1=t1s[e][:], op0=ALU.mult, op1=ALU.add,
-                    )
-            if b == 0:
-                prepare_w()
-            grouped = stage.tile([P, TOK, 4], BF16, align_bytes=64)
-            nc.gpsimd.tensor_scalar(
-                out=grouped[:], in0=planes[:].rearrange("q t n -> q n t"),
-                scalar1=1.0, scalar2=0.0, op0=ALU.mult, op1=ALU.add,
-            )
-            codes = stage.tile([P, TOK], U32, align_bytes=64)
-            scales = stage.tile([P, TOK], U8, align_bytes=64)
-            nc.vector.quantize_mx(
-                out=codes[:].bitcast(FP8X4), scales=scales[:],
-                in_=grouped[:].rearrange("q n t -> q (n t)"),
-            )
-            o_sb = stage.tile([P, 4, TOK], F32)
+        banks = {}
+        t0s = {}
+        t1s = {}
+        planes = {}
+        grouped = {}
+        codes = {}
+        scales = {}
+
+        def gate_of(n, k, e):
+            return gate[:, 8 * (n % 2) + n // 2, k, e : e + 1]
+
+        def transposes(n, k):
+            if n >= UNITS:
+                return
+            b, u = n // 2, n % 2
+            bank = psum.tile([P, 4, P], F32, name="bank%d" % k, tag="t%d" % k)
+            xw = x_sb[b][k][:].bitcast(F32)
             for j in range(4):
-                acc = psum.tile([P, TOK], F32, tag="o")
+                nc.tensor.transpose(bank[:, j, :], xw[:, j, P * u : P * u + P], ident[:])
+            banks[(n, k)] = bank
+
+        def pass1(n):
+            if n >= UNITS:
+                return
+            for e in range(2):
+                t0 = work.tile([P, P, 4], F32, name="t0", bufs=8)
+                nc.scalar.activation(
+                    out=t0[:], in_=half_view(banks[(n, 0)], e), func=ACT.Copy, scale=gate_of(n, 0, e)
+                )
+                t0s[(n, e)] = t0
+
+        def pass2(n):
+            for e in range(2):
+                t1 = work.tile([P, P, 4], F32, name="t1")
+                nc.vector.scalar_tensor_tensor(
+                    out=t1[:], in0=half_view(banks[(n, 1)], e), scalar=gate_of(n, 1, e),
+                    in1=t0s[(n, e)][:], op0=ALU.mult, op1=ALU.add,
+                )
+                t1s[(n, e)] = t1
+
+        def pass3(n):
+            b, u = n // 2, n % 2
+            if u == 0:
+                planes[b] = stage.tile([P, 4, TOK], BF16, name="planes")
+            for e in range(2):
+                nc.vector.scalar_tensor_tensor(
+                    out=planes[b][:, 2 * u + e, :].rearrange("q (p j) -> q p j", j=4),
+                    in0=half_view(banks[(n, 2)], e), scalar=gate_of(n, 2, e),
+                    in1=t1s[(n, e)][:], op0=ALU.mult, op1=ALU.add,
+                )
+
+        def regroup(b):
+            g = stage.tile([P, TOK, 4], BF16, name="grouped", align_bytes=64)
+            grouped[b] = g
+            src = planes[b][:].rearrange("q t n -> q n t")
+            if b < B - 1:
+                nc.gpsimd.tensor_scalar(
+                    out=g[:], in0=src, scalar1=1.0, scalar2=0.0, op0=ALU.mult, op1=ALU.add
+                )
+            else:
+                nc.vector.tensor_copy(out=g[:, 0:256, :], in_=src[:, 0:256, :])
+                nc.scalar.copy(out=g[:, 256:384, :], in_=src[:, 256:384, :])
+                nc.gpsimd.tensor_scalar(
+                    out=g[:, 384:512, :], in0=src[:, 384:512, :], scalar1=1.0, scalar2=0.0,
+                    op0=ALU.mult, op1=ALU.add,
+                )
+
+        def quantise(b):
+            codes[b] = stage.tile([P, TOK], U32, name="codes", align_bytes=64)
+            scales[b] = stage.tile([P, TOK], U8, name="scales", align_bytes=64)
+            nc.vector.quantize_mx(
+                out=codes[b][:].bitcast(FP8X4), scales=scales[b][:],
+                in_=grouped[b][:].rearrange("q n t -> q (n t)"),
+            )
+
+        def project(b):
+            last = b == B - 1
+            o_sb = stage.tile([P, 4, TOK], F32, name="o_sb")
+            dst = out[b].rearrange("(i j) w h -> i j (w h)", j=4)
+            for j in range(4):
+                acc = psum.tile([P, TOK], F32, name="acc", tag="o")
                 nc.tensor.matmul_mx(
                     out=acc[:],
                     lhsT=w_codes[:, P * j : P * j + P].bitcast(FP8X4),
                     lhsT_scale=w_scales[:, P * j : P * j + P],
-                    rhs=codes[:].bitcast(FP8X4),
-                    rhs_scale=scales[:],
+                    rhs=codes[b][:].bitcast(FP8X4),
+                    rhs_scale=scales[b][:],
                     start=True,
                     stop=True,
                 )
-                nc.scalar.activation(
-                    out=o_sb[:, j, :], in_=acc[:], func=ACT.Identity, bias=b2_f[:, j : j + 1], scale=1.0
-                )
-            nc.scalar.dma_start(
-                out=out[b].rearrange("(i j) w h -> i (j w h)", j=4),
-                in_=o_sb[:].rearrange("i j n -> i (j n)"),
-            )
+                if last and j % 2 == 1:
+                    nc.vector.tensor_scalar_add(out=o_sb[:, j, :], in0=acc[:], scalar1=b2_f[:, j : j + 1])
+                else:
+                    nc.scalar.activation(
+                        out=o_sb[:, j, :], in_=acc[:], func=ACT.Identity, bias=b2_f[:, j : j + 1],
+                        scale=1.0,
+                    )
+                if last and j == 1:
+                    nc.sync.dma_start(out=dst[:, 0:2, :], in_=o_sb[:, 0:2, :])
+            if last:
+                nc.scalar.dma_start(out=dst[:, 2:4, :], in_=o_sb[:, 2:4, :])
+            else:
+                nc.scalar.dma_start(out=dst, in_=o_sb[:])
+
+        for n in range(2):
+            for k in range(3):
+                transposes(n, k)
+            pass1(n)
+        transposes(2, 0)
+        pass1(2)
+        for n in range(UNITS):
+            pass2(n)
+            transposes(n + 2, 1)
+            if n == 2:
+                transpose_w()
+            if n % 2 == 1 and n >= 3:
+                quantise((n - 3) // 2)
+                project((n - 3) // 2)
+            pass3(n)
+            if n == 2:
+                nc.vector.quantize_mx(out=w_codes[:].bitcast(FP8X4), scales=w_scales[:], in_=w_grouped[:])
+            transposes(n + 2, 2)
+            transposes(n + 3, 0)
+            pass1(n + 3)
+            if n % 2 == 1:
+                regroup(n // 2)
+        quantise(B - 1)
+        project(B - 1)

@@ -17,6 +17,7 @@ B = 8
 C = 512
 TOK = 512
 UNITS = 2 * B
+REPEAT = 2
 FLOPS = 2 * B * TOK * C * C
 
 
@@ -193,21 +194,26 @@ def tile_modelnew_pb_t_kernel(tc, x1, x2, x3, hat, w2, b2, out):
                 in_=grouped[b][:].rearrange("q n t -> q (n t)"),
             )
 
-        def project(b):
+        o_sbs = {}
+
+        def project(b, js, repeat):
             last = b == B - 1
-            o_sb = stage.tile([P, 4, TOK], F32, name="o_sb")
+            if js[0] == 0:
+                o_sbs[b] = stage.tile([P, 4, TOK], F32, name="o_sb")
+            o_sb = o_sbs[b]
             dst = out[b].rearrange("(i j) w h -> i j (w h)", j=4)
-            for j in range(4):
+            for j in js:
                 acc = psum.tile([P, TOK], F32, name="acc", tag="o")
-                nc.tensor.matmul_mx(
-                    out=acc[:],
-                    lhsT=w_codes[:, P * j : P * j + P].bitcast(FP8X4),
-                    lhsT_scale=w_scales[:, P * j : P * j + P],
-                    rhs=codes[b][:].bitcast(FP8X4),
-                    rhs_scale=scales[b][:],
-                    start=True,
-                    stop=True,
-                )
+                for r in range(repeat):
+                    nc.tensor.matmul_mx(
+                        out=acc[:],
+                        lhsT=w_codes[:, P * j : P * j + P].bitcast(FP8X4),
+                        lhsT_scale=w_scales[:, P * j : P * j + P],
+                        rhs=codes[b][:].bitcast(FP8X4),
+                        rhs_scale=scales[b][:],
+                        start=True,
+                        stop=True,
+                    )
                 if last and j % 2 == 1:
                     nc.vector.tensor_scalar_add(out=o_sb[:, j, :], in0=acc[:], scalar1=b2_f[:, j : j + 1])
                 else:
@@ -215,11 +221,10 @@ def tile_modelnew_pb_t_kernel(tc, x1, x2, x3, hat, w2, b2, out):
                         out=o_sb[:, j, :], in_=acc[:], func=ACT.Identity, bias=b2_f[:, j : j + 1],
                         scale=1.0,
                     )
-                if last and j == 1:
-                    nc.sync.dma_start(out=dst[:, 0:2, :], in_=o_sb[:, 0:2, :])
             if last:
-                nc.scalar.dma_start(out=dst[:, 2:4, :], in_=o_sb[:, 2:4, :])
-            else:
+                eng = nc.sync if js[0] == 0 else nc.scalar
+                eng.dma_start(out=dst[:, js[0] : js[0] + 2, :], in_=o_sb[:, js[0] : js[0] + 2, :])
+            elif js[0] == 2:
                 nc.scalar.dma_start(out=dst, in_=o_sb[:])
 
         for n in range(2):
@@ -229,20 +234,25 @@ def tile_modelnew_pb_t_kernel(tc, x1, x2, x3, hat, w2, b2, out):
         transposes(2, 0)
         pass1(2)
         for n in range(UNITS):
+            transposes(n + 3, 0)
+            pass1(n + 3)
             pass2(n)
             transposes(n + 2, 1)
             if n == 2:
                 transpose_w()
-            if n % 2 == 1 and n >= 3:
-                quantise((n - 3) // 2)
-                project((n - 3) // 2)
+            if n >= 3:
+                if n % 2 == 1:
+                    quantise((n - 3) // 2)
+                    project((n - 3) // 2, [0, 1], REPEAT)
+                else:
+                    project((n - 4) // 2, [2, 3], REPEAT)
             pass3(n)
             if n == 2:
                 nc.vector.quantize_mx(out=w_codes[:].bitcast(FP8X4), scales=w_scales[:], in_=w_grouped[:])
             transposes(n + 2, 2)
-            transposes(n + 3, 0)
-            pass1(n + 3)
             if n % 2 == 1:
                 regroup(n // 2)
+        project(B - 2, [2, 3], 1)
         quantise(B - 1)
-        project(B - 1)
+        project(B - 1, [0, 1], 1)
+        project(B - 1, [2, 3], 1)

@@ -18,6 +18,7 @@ C = 512
 TOK = 512
 UNITS = 2 * B
 REPEAT = 2
+VECTOR_OUT = [3]
 FLOPS = 2 * B * TOK * C * C
 
 
@@ -28,7 +29,7 @@ def tile_modelnew_pb_t_kernel(tc, x1, x2, x3, hat, w2, b2, out):
         const = ctx.enter_context(tc.tile_pool(name="const", bufs=1))
         xin = ctx.enter_context(tc.tile_pool(name="xin", bufs=B))
         work = ctx.enter_context(tc.tile_pool(name="work", bufs=4))
-        stage = ctx.enter_context(tc.tile_pool(name="stage", bufs=3))
+        stage = ctx.enter_context(tc.tile_pool(name="stage", bufs=4))
         psum = ctx.enter_context(tc.psum_pool(name="psum", bufs=2))
         ctx.enter_context(tc.manual_schedule())
 
@@ -195,15 +196,29 @@ def tile_modelnew_pb_t_kernel(tc, x1, x2, x3, hat, w2, b2, out):
             )
 
         o_sbs = {}
+        accs = {}
 
-        def project(b, js, repeat):
-            last = b == B - 1
+        def way_out(b, j, on_vector):
+            if on_vector:
+                nc.vector.tensor_scalar_add(
+                    out=o_sbs[b][:, j, :], in0=accs[(b, j)][:], scalar1=b2_f[:, j : j + 1]
+                )
+            else:
+                nc.scalar.activation(
+                    out=o_sbs[b][:, j, :], in_=accs[(b, j)][:], func=ACT.Identity,
+                    bias=b2_f[:, j : j + 1], scale=1.0,
+                )
+
+        def store(b, j0, j1, eng):
+            dst = out[b].rearrange("(i j) w h -> i j (w h)", j=4)
+            eng.dma_start(out=dst[:, j0:j1, :], in_=o_sbs[b][:, j0:j1, :])
+
+        def passes(b, js, repeat):
             if js[0] == 0:
                 o_sbs[b] = stage.tile([P, 4, TOK], F32, name="o_sb")
-            o_sb = o_sbs[b]
-            dst = out[b].rearrange("(i j) w h -> i j (w h)", j=4)
             for j in js:
                 acc = psum.tile([P, TOK], F32, name="acc", tag="o")
+                accs[(b, j)] = acc
                 for r in range(repeat):
                     nc.tensor.matmul_mx(
                         out=acc[:],
@@ -214,18 +229,8 @@ def tile_modelnew_pb_t_kernel(tc, x1, x2, x3, hat, w2, b2, out):
                         start=True,
                         stop=True,
                     )
-                if last and j % 2 == 1:
-                    nc.vector.tensor_scalar_add(out=o_sb[:, j, :], in0=acc[:], scalar1=b2_f[:, j : j + 1])
-                else:
-                    nc.scalar.activation(
-                        out=o_sb[:, j, :], in_=acc[:], func=ACT.Identity, bias=b2_f[:, j : j + 1],
-                        scale=1.0,
-                    )
-            if last:
-                eng = nc.sync if js[0] == 0 else nc.scalar
-                eng.dma_start(out=dst[:, js[0] : js[0] + 2, :], in_=o_sb[:, js[0] : js[0] + 2, :])
-            elif js[0] == 2:
-                nc.scalar.dma_start(out=dst, in_=o_sb[:])
+                if j not in VECTOR_OUT:
+                    way_out(b, j, False)
 
         for n in range(2):
             for k in range(3):
@@ -242,17 +247,39 @@ def tile_modelnew_pb_t_kernel(tc, x1, x2, x3, hat, w2, b2, out):
                 transpose_w()
             if n >= 3:
                 if n % 2 == 1:
+                    if n >= 5:
+                        for j in VECTOR_OUT:
+                            way_out((n - 5) // 2, j, True)
+                        store((n - 5) // 2, 0, 4, nc.scalar)
                     quantise((n - 3) // 2)
-                    project((n - 3) // 2, [0, 1], REPEAT)
+                    passes((n - 3) // 2, [0, 1], REPEAT)
                 else:
-                    project((n - 4) // 2, [2, 3], REPEAT)
+                    passes((n - 4) // 2, [2, 3], REPEAT)
             pass3(n)
             if n == 2:
                 nc.vector.quantize_mx(out=w_codes[:].bitcast(FP8X4), scales=w_scales[:], in_=w_grouped[:])
             transposes(n + 2, 2)
             if n % 2 == 1:
                 regroup(n // 2)
-        project(B - 2, [2, 3], 1)
+        passes(B - 2, [2, 3], 1)
+        for j in VECTOR_OUT:
+            way_out(B - 2, j, True)
+        store(B - 2, 0, 4, nc.scalar)
         quantise(B - 1)
-        project(B - 1, [0, 1], 1)
-        project(B - 1, [2, 3], 1)
+        o_sbs[B - 1] = stage.tile([P, 4, TOK], F32, name="o_sb")
+        for j in range(4):
+            acc = psum.tile([P, TOK], F32, name="acc", tag="o")
+            accs[(B - 1, j)] = acc
+            nc.tensor.matmul_mx(
+                out=acc[:],
+                lhsT=w_codes[:, P * j : P * j + P].bitcast(FP8X4),
+                lhsT_scale=w_scales[:, P * j : P * j + P],
+                rhs=codes[B - 1][:].bitcast(FP8X4),
+                rhs_scale=scales[B - 1][:],
+                start=True,
+                stop=True,
+            )
+            way_out(B - 1, j, j % 2 == 1)
+            if j == 1:
+                store(B - 1, 0, 2, nc.sync)
+        store(B - 1, 2, 4, nc.scalar)

@@ -17,9 +17,8 @@ B = 8
 C = 512
 TOK = 512
 UNITS = 2 * B
-REPEAT = 2
-VECTOR_OUT = [3]
 FLOPS = 2 * B * TOK * C * C
+REPEAT = 2
 
 
 def tile_modelnew_pb_t_kernel(tc, x1, x2, x3, hat, w2, b2, out):
@@ -51,6 +50,7 @@ def tile_modelnew_pb_t_kernel(tc, x1, x2, x3, hat, w2, b2, out):
         make_identity(nc, ident[:])
 
         w_sb = const.tile([P, 4, C], BF16)
+        nc.sync.dma_start(out=w_sb[:], in_=w2.rearrange("(i j) c -> i j c", j=4))
         x_sb = []
         for b in range(B):
             row = []
@@ -60,8 +60,6 @@ def tile_modelnew_pb_t_kernel(tc, x1, x2, x3, hat, w2, b2, out):
                 nc.sync.dma_start(out=xt[:], in_=src)
                 row.append(xt)
             x_sb.append(row)
-            if b == 1:
-                nc.sync.dma_start(out=w_sb[:], in_=w2.rearrange("(i j) c -> i j c", j=4))
 
         aux_ps = psum.tile([P, 2, P], F32, tag="o")
         hat_w = hat_sb[:].bitcast(F32)
@@ -94,27 +92,26 @@ def tile_modelnew_pb_t_kernel(tc, x1, x2, x3, hat, w2, b2, out):
             out=gate[:], in0=expd[:], in1=inv[:].unsqueeze(2).to_broadcast([P, 16, 3, 2]),
             op=ALU.mult,
         )
-        b2_f = const.tile([P, 4], F32)
-        nc.vector.tensor_copy(out=b2_f[:], in_=b2_bf[:])
 
         w_codes = const.tile([P, C], U32, align_bytes=64)
         w_scales = const.tile([P, C], U8, align_bytes=64)
         w_grouped = const.tile([P, 4 * C], BF16, align_bytes=64)
-
-        def transpose_w():
-            w_words = w_sb[:].bitcast(F32)
-            w_pairs = w_grouped[:].bitcast(F32).rearrange("q (c u) -> q c u", u=2)
-            for h in range(2):
-                w_ps = psum.tile([P, 2, 2, P], F32, tag="o")
-                for u in range(2):
-                    for jj in range(2):
-                        nc.tensor.transpose(
-                            w_ps[:, u, jj, :], w_words[:, 2 * h + jj, P * u : P * u + P], ident[:]
-                        )
-                nc.scalar.copy(
-                    out=w_pairs[:, 256 * h : 256 * h + 256, :],
-                    in_=w_ps[:].rearrange("q u jj i -> q (jj i) u"),
-                )
+        w_words = w_sb[:].bitcast(F32)
+        w_pairs = w_grouped[:].bitcast(F32).rearrange("q (c u) -> q c u", u=2)
+        for h in range(2):
+            w_ps = psum.tile([P, 2, 2, P], F32, tag="o")
+            for u in range(2):
+                for jj in range(2):
+                    nc.tensor.transpose(
+                        w_ps[:, u, jj, :], w_words[:, 2 * h + jj, P * u : P * u + P], ident[:]
+                    )
+            nc.vector.tensor_copy(
+                out=w_pairs[:, 256 * h : 256 * h + 256, :],
+                in_=w_ps[:].rearrange("q u jj i -> q (jj i) u"),
+            )
+        b2_f = const.tile([P, 4], F32)
+        nc.vector.tensor_copy(out=b2_f[:], in_=b2_bf[:])
+        nc.vector.quantize_mx(out=w_codes[:].bitcast(FP8X4), scales=w_scales[:], in_=w_grouped[:])
 
         def half_view(bank, e):
             v = bank[:].bitcast(BF16).rearrange("q j (p e) -> q j p e", e=2)
@@ -127,6 +124,7 @@ def tile_modelnew_pb_t_kernel(tc, x1, x2, x3, hat, w2, b2, out):
         grouped = {}
         codes = {}
         scales = {}
+        o_sbs = {}
 
         def gate_of(n, k, e):
             return gate[:, 8 * (n % 2) + n // 2, k, e : e + 1]
@@ -175,17 +173,13 @@ def tile_modelnew_pb_t_kernel(tc, x1, x2, x3, hat, w2, b2, out):
             g = stage.tile([P, TOK, 4], BF16, name="grouped", align_bytes=64)
             grouped[b] = g
             src = planes[b][:].rearrange("q t n -> q n t")
-            if b < B - 1:
-                nc.gpsimd.tensor_scalar(
-                    out=g[:], in0=src, scalar1=1.0, scalar2=0.0, op0=ALU.mult, op1=ALU.add
-                )
-            else:
-                nc.vector.tensor_copy(out=g[:, 0:256, :], in_=src[:, 0:256, :])
-                nc.scalar.copy(out=g[:, 256:384, :], in_=src[:, 256:384, :])
-                nc.gpsimd.tensor_scalar(
-                    out=g[:, 384:512, :], in0=src[:, 384:512, :], scalar1=1.0, scalar2=0.0,
-                    op0=ALU.mult, op1=ALU.add,
-                )
+            cut = 0 if b < B - 1 else 384
+            if cut:
+                nc.vector.tensor_copy(out=g[:, 0:cut, :], in_=src[:, 0:cut, :])
+            nc.gpsimd.tensor_scalar(
+                out=g[:, cut:TOK, :], in0=src[:, cut:TOK, :], scalar1=1.0, scalar2=0.0,
+                op0=ALU.mult, op1=ALU.add,
+            )
 
         def quantise(b):
             codes[b] = stage.tile([P, TOK], U32, name="codes", align_bytes=64)
@@ -195,31 +189,15 @@ def tile_modelnew_pb_t_kernel(tc, x1, x2, x3, hat, w2, b2, out):
                 in_=grouped[b][:].rearrange("q n t -> q (n t)"),
             )
 
-        o_sbs = {}
-        accs = {}
-
-        def way_out(b, j, on_vector):
-            if on_vector:
-                nc.vector.tensor_scalar_add(
-                    out=o_sbs[b][:, j, :], in0=accs[(b, j)][:], scalar1=b2_f[:, j : j + 1]
-                )
-            else:
-                nc.scalar.activation(
-                    out=o_sbs[b][:, j, :], in_=accs[(b, j)][:], func=ACT.Identity,
-                    bias=b2_f[:, j : j + 1], scale=1.0,
-                )
-
-        def store(b, j0, j1, eng):
-            dst = out[b].rearrange("(i j) w h -> i j (w h)", j=4)
-            eng.dma_start(out=dst[:, j0:j1, :], in_=o_sbs[b][:, j0:j1, :])
-
-        def passes(b, js, repeat):
-            if js[0] == 0:
+        def project(b, j0):
+            last = b == B - 1
+            if j0 == 0:
                 o_sbs[b] = stage.tile([P, 4, TOK], F32, name="o_sb")
-            for j in js:
-                acc = psum.tile([P, TOK], F32, name="acc", tag="o")
-                accs[(b, j)] = acc
-                for r in range(repeat):
+            o_sb = o_sbs[b]
+            for j in (j0, j0 + 1):
+                tag = "t%d" % (j - 2) if last and j >= 2 else "o"
+                acc = psum.tile([P, TOK], F32, name="acc", tag=tag)
+                for r in range(1 if b >= B - 2 and (last or j0 == 2) else REPEAT):
                     nc.tensor.matmul_mx(
                         out=acc[:],
                         lhsT=w_codes[:, P * j : P * j + P].bitcast(FP8X4),
@@ -229,8 +207,16 @@ def tile_modelnew_pb_t_kernel(tc, x1, x2, x3, hat, w2, b2, out):
                         start=True,
                         stop=True,
                     )
-                if j not in VECTOR_OUT:
-                    way_out(b, j, False)
+                if last and j % 2 == 1:
+                    nc.vector.tensor_scalar_add(out=o_sb[:, j, :], in0=acc[:], scalar1=b2_f[:, j : j + 1])
+                else:
+                    nc.scalar.activation(
+                        out=o_sb[:, j, :], in_=acc[:], func=ACT.Identity, bias=b2_f[:, j : j + 1],
+                        scale=1.0,
+                    )
+            dst = out[b].rearrange("(i j) w h -> i j (w h)", j=4)
+            eng = nc.sync if last and j0 == 0 else nc.scalar
+            eng.dma_start(out=dst[:, j0 : j0 + 2, :], in_=o_sb[:, j0 : j0 + 2, :])
 
         for n in range(2):
             for k in range(3):
@@ -241,45 +227,18 @@ def tile_modelnew_pb_t_kernel(tc, x1, x2, x3, hat, w2, b2, out):
         for n in range(UNITS):
             transposes(n + 3, 0)
             pass1(n + 3)
+            if n % 2 == 0 and n >= 4:
+                project((n - 4) // 2, 2)
             pass2(n)
             transposes(n + 2, 1)
-            if n == 2:
-                transpose_w()
-            if n >= 3:
-                if n % 2 == 1:
-                    if n >= 5:
-                        for j in VECTOR_OUT:
-                            way_out((n - 5) // 2, j, True)
-                        store((n - 5) // 2, 0, 4, nc.scalar)
-                    quantise((n - 3) // 2)
-                    passes((n - 3) // 2, [0, 1], REPEAT)
-                else:
-                    passes((n - 4) // 2, [2, 3], REPEAT)
+            if n % 2 == 1 and n >= 3:
+                quantise((n - 3) // 2)
+                project((n - 3) // 2, 0)
             pass3(n)
-            if n == 2:
-                nc.vector.quantize_mx(out=w_codes[:].bitcast(FP8X4), scales=w_scales[:], in_=w_grouped[:])
             transposes(n + 2, 2)
             if n % 2 == 1:
                 regroup(n // 2)
-        passes(B - 2, [2, 3], 1)
-        for j in VECTOR_OUT:
-            way_out(B - 2, j, True)
-        store(B - 2, 0, 4, nc.scalar)
+        project(B - 2, 2)
         quantise(B - 1)
-        o_sbs[B - 1] = stage.tile([P, 4, TOK], F32, name="o_sb")
-        for j in range(4):
-            acc = psum.tile([P, TOK], F32, name="acc", tag="o")
-            accs[(B - 1, j)] = acc
-            nc.tensor.matmul_mx(
-                out=acc[:],
-                lhsT=w_codes[:, P * j : P * j + P].bitcast(FP8X4),
-                lhsT_scale=w_scales[:, P * j : P * j + P],
-                rhs=codes[B - 1][:].bitcast(FP8X4),
-                rhs_scale=scales[B - 1][:],
-                start=True,
-                stop=True,
-            )
-            way_out(B - 1, j, j % 2 == 1)
-            if j == 1:
-                store(B - 1, 0, 2, nc.sync)
-        store(B - 1, 2, 4, nc.scalar)
+        project(B - 1, 0)
+        project(B - 1, 2)

@@ -18,7 +18,7 @@ C = 512
 TOK = 512
 UNITS = 2 * B
 FLOPS = 2 * B * TOK * C * C
-REPEAT = 2
+REPEAT = 1
 
 
 def tile_modelnew_pb_t_kernel(tc, x1, x2, x3, hat, w2, b2, out):

@@ -18,7 +18,6 @@ C = 512
 TOK = 512
 UNITS = 2 * B
 FLOPS = 2 * B * TOK * C * C
-REPEAT = 1
 
 
 def tile_modelnew_pb_t_kernel(tc, x1, x2, x3, hat, w2, b2, out):
@@ -149,14 +148,13 @@ def tile_modelnew_pb_t_kernel(tc, x1, x2, x3, hat, w2, b2, out):
                 )
                 t0s[(n, e)] = t0
 
-        def pass2(n):
-            for e in range(2):
-                t1 = work.tile([P, P, 4], F32, name="t1")
-                nc.vector.scalar_tensor_tensor(
-                    out=t1[:], in0=half_view(banks[(n, 1)], e), scalar=gate_of(n, 1, e),
-                    in1=t0s[(n, e)][:], op0=ALU.mult, op1=ALU.add,
-                )
-                t1s[(n, e)] = t1
+        def pass2(n, e):
+            t1 = work.tile([P, P, 4], F32, name="t1")
+            nc.vector.scalar_tensor_tensor(
+                out=t1[:], in0=half_view(banks[(n, 1)], e), scalar=gate_of(n, 1, e),
+                in1=t0s[(n, e)][:], op0=ALU.mult, op1=ALU.add,
+            )
+            t1s[(n, e)] = t1
 
         def pass3(n):
             b, u = n // 2, n % 2
@@ -170,53 +168,55 @@ def tile_modelnew_pb_t_kernel(tc, x1, x2, x3, hat, w2, b2, out):
                 )
 
         def regroup(b):
-            g = stage.tile([P, TOK, 4], BF16, name="grouped", align_bytes=64)
-            grouped[b] = g
-            src = planes[b][:].rearrange("q t n -> q n t")
-            cut = 0 if b < B - 1 else 384
-            if cut:
-                nc.vector.tensor_copy(out=g[:, 0:cut, :], in_=src[:, 0:cut, :])
+            grouped[b] = stage.tile([P, TOK, 4], BF16, name="grouped", align_bytes=64)
             nc.gpsimd.tensor_scalar(
-                out=g[:, cut:TOK, :], in0=src[:, cut:TOK, :], scalar1=1.0, scalar2=0.0,
-                op0=ALU.mult, op1=ALU.add,
+                out=grouped[b][:], in0=planes[b][:].rearrange("q t n -> q n t"), scalar1=1.0,
+                scalar2=0.0, op0=ALU.mult, op1=ALU.add,
             )
 
-        def quantise(b):
-            codes[b] = stage.tile([P, TOK], U32, name="codes", align_bytes=64)
-            scales[b] = stage.tile([P, TOK], U8, name="scales", align_bytes=64)
+        def quantise(b, lo, hi):
+            if lo == 0:
+                codes[b] = stage.tile([P, TOK], U32, name="codes", align_bytes=64)
+                scales[b] = stage.tile([P, TOK], U8, name="scales", align_bytes=64)
             nc.vector.quantize_mx(
-                out=codes[b][:].bitcast(FP8X4), scales=scales[b][:],
-                in_=grouped[b][:].rearrange("q n t -> q (n t)"),
+                out=codes[b][:, lo:hi].bitcast(FP8X4), scales=scales[b][:, lo:hi],
+                in_=grouped[b][:, lo:hi, :].rearrange("q n t -> q (n t)"),
             )
 
-        def project(b, j0):
-            last = b == B - 1
+        def one_pass(b, j, lo, hi, tag):
+            acc = psum.tile([P, hi - lo], F32, name="acc", tag=tag)
+            nc.tensor.matmul_mx(
+                out=acc[:],
+                lhsT=w_codes[:, P * j : P * j + P].bitcast(FP8X4),
+                lhsT_scale=w_scales[:, P * j : P * j + P],
+                rhs=codes[b][:, lo:hi].bitcast(FP8X4),
+                rhs_scale=scales[b][:, lo:hi],
+                start=True,
+                stop=True,
+            )
+            return acc
+
+        def way_out(b, j, lo, hi, acc, on_vector):
+            if on_vector:
+                nc.vector.tensor_scalar_add(
+                    out=o_sbs[b][:, j, lo:hi], in0=acc[:], scalar1=b2_f[:, j : j + 1]
+                )
+            else:
+                nc.scalar.activation(
+                    out=o_sbs[b][:, j, lo:hi], in_=acc[:], func=ACT.Identity,
+                    bias=b2_f[:, j : j + 1], scale=1.0,
+                )
+
+        def store(b, j0, lo, hi, eng):
+            dst = out[b].rearrange("(i j) w h -> i j (w h)", j=4)
+            eng.dma_start(out=dst[:, j0 : j0 + 2, lo:hi], in_=o_sbs[b][:, j0 : j0 + 2, lo:hi])
+
+        def project(b, j0, tag):
             if j0 == 0:
                 o_sbs[b] = stage.tile([P, 4, TOK], F32, name="o_sb")
-            o_sb = o_sbs[b]
             for j in (j0, j0 + 1):
-                tag = "t%d" % (j - 2) if last and j >= 2 else "o"
-                acc = psum.tile([P, TOK], F32, name="acc", tag=tag)
-                for r in range(1 if b >= B - 2 and (last or j0 == 2) else REPEAT):
-                    nc.tensor.matmul_mx(
-                        out=acc[:],
-                        lhsT=w_codes[:, P * j : P * j + P].bitcast(FP8X4),
-                        lhsT_scale=w_scales[:, P * j : P * j + P],
-                        rhs=codes[b][:].bitcast(FP8X4),
-                        rhs_scale=scales[b][:],
-                        start=True,
-                        stop=True,
-                    )
-                if last and j % 2 == 1:
-                    nc.vector.tensor_scalar_add(out=o_sb[:, j, :], in0=acc[:], scalar1=b2_f[:, j : j + 1])
-                else:
-                    nc.scalar.activation(
-                        out=o_sb[:, j, :], in_=acc[:], func=ACT.Identity, bias=b2_f[:, j : j + 1],
-                        scale=1.0,
-                    )
-            dst = out[b].rearrange("(i j) w h -> i j (w h)", j=4)
-            eng = nc.sync if last and j0 == 0 else nc.scalar
-            eng.dma_start(out=dst[:, j0 : j0 + 2, :], in_=o_sb[:, j0 : j0 + 2, :])
+                way_out(b, j, 0, TOK, one_pass(b, j, 0, TOK, tag), False)
+            store(b, j0, 0, TOK, nc.scalar)
 
         for n in range(2):
             for k in range(3):
@@ -228,17 +228,40 @@ def tile_modelnew_pb_t_kernel(tc, x1, x2, x3, hat, w2, b2, out):
             transposes(n + 3, 0)
             pass1(n + 3)
             if n % 2 == 0 and n >= 4:
-                project((n - 4) // 2, 2)
-            pass2(n)
+                project((n - 4) // 2, 2, "o")
+            pass2(n, 0)
+            if n == UNITS - 1:
+                quantise(B - 2, 0, TOK)
+                project(B - 2, 0, "o")
+                project(B - 2, 2, "t0")
+            pass2(n, 1)
             transposes(n + 2, 1)
-            if n % 2 == 1 and n >= 3:
-                quantise((n - 3) // 2)
-                project((n - 3) // 2, 0)
+            if n % 2 == 1 and 3 <= n < UNITS - 1:
+                quantise((n - 3) // 2, 0, TOK)
+                project((n - 3) // 2, 0, "o")
             pass3(n)
             transposes(n + 2, 2)
-            if n % 2 == 1:
+            if n % 2 == 1 and n < UNITS - 1:
                 regroup(n // 2)
-        project(B - 2, 2)
-        quantise(B - 1)
-        project(B - 1, 0)
-        project(B - 1, 2)
+
+        b = B - 1
+        HALF = TOK // 2
+        g = stage.tile([P, TOK, 4], BF16, name="grouped", align_bytes=64)
+        grouped[b] = g
+        src = planes[b][:].rearrange("q t n -> q n t")
+        nc.vector.tensor_copy(out=g[:, 0:HALF, :], in_=src[:, 0:HALF, :])
+        nc.gpsimd.tensor_scalar(
+            out=g[:, 384:TOK, :], in0=src[:, 384:TOK, :], scalar1=1.0, scalar2=0.0,
+            op0=ALU.mult, op1=ALU.add,
+        )
+        nc.vector.tensor_copy(out=g[:, HALF:384, :], in_=src[:, HALF:384, :])
+        quantise(b, 0, HALF)
+        quantise(b, HALF, TOK)
+        o_sbs[b] = stage.tile([P, 4, TOK], F32, name="o_sb")
+        for h, tags in ((0, ("t1", "t1", "t2", "t2")), (1, ("o", "o", "t0", "t0"))):
+            lo, hi = h * HALF, h * HALF + HALF
+            accs = [one_pass(b, j, lo, hi, tags[j]) for j in range(4)]
+            for j in range(4):
+                way_out(b, j, lo, hi, accs[j], j % 2 == 1)
+                if j % 2 == 1:
+                    store(b, j - 1, lo, hi, nc.sync)

@@ -33,7 +33,8 @@ def tile_modelnew_pb_t_kernel(tc, x1, x2, x3, hat, w2, b2, out):
 
         hat_sb = const.tile([P, C], BF16)
         hat_rows = hat.rearrange("b (k c) -> (b k) c", k=3)
-        nc.sync.dma_start(out=hat_sb[0:24, :], in_=hat_rows)
+        nc.sync.dma_start(out=hat_sb[0:16, :], in_=hat_rows[0:16, :])
+        nc.scalar.dma_start(out=hat_sb[16:24, :], in_=hat_rows[16:24, :])
         nc.scalar.dma_start(out=hat_sb[24:32, :], in_=hat_rows[0:8, :])
         nc.vector.memset(hat_sb[32:64, :], 0.0)
         nc.vector.memset(hat_sb[64:128, :], 0.0)
@@ -104,7 +105,8 @@ def tile_modelnew_pb_t_kernel(tc, x1, x2, x3, hat, w2, b2, out):
                     nc.tensor.transpose(
                         w_ps[:, u, jj, :], w_words[:, 2 * h + jj, P * u : P * u + P], ident[:]
                     )
-            nc.vector.tensor_copy(
+            copy = nc.vector.tensor_copy if h == 0 else nc.scalar.copy
+            copy(
                 out=w_pairs[:, 256 * h : 256 * h + 256, :],
                 in_=w_ps[:].rearrange("q u jj i -> q (jj i) u"),
             )

from contextlib import ExitStack

import concourse.mybir as mybir
from concourse.masks import make_identity

F32 = mybir.dt.float32
BF16 = mybir.dt.bfloat16
U32 = mybir.dt.uint32
U8 = mybir.dt.uint8
FP8X4 = mybir.dt.float8_e4m3fn_x4
ALU = mybir.AluOpType
ACT = mybir.ActivationFunctionType
AX = mybir.AxisListType

P = 128
B = 8
C = 512
TOK = 512
UNITS = 2 * B
FLOPS = 2 * B * TOK * C * C


def tile_modelnew_pb_t_kernel(tc, x1, x2, x3, hat, w2, b2, out):
    nc = tc.nc
    xs = [x1, x2, x3]
    with ExitStack() as ctx:
        const = ctx.enter_context(tc.tile_pool(name="const", bufs=1))
        xin = ctx.enter_context(tc.tile_pool(name="xin", bufs=B))
        work = ctx.enter_context(tc.tile_pool(name="work", bufs=4))
        stage = ctx.enter_context(tc.tile_pool(name="stage", bufs=4))
        psum = ctx.enter_context(tc.psum_pool(name="psum", bufs=2))
        ctx.enter_context(tc.manual_schedule())

        hat_sb = const.tile([P, C], BF16)
        hat_rows = hat.rearrange("b (k c) -> (b k) c", k=3)
        nc.sync.dma_start(out=hat_sb[0:16, :], in_=hat_rows[0:16, :])
        nc.scalar.dma_start(out=hat_sb[16:24, :], in_=hat_rows[16:24, :])
        nc.scalar.dma_start(out=hat_sb[24:32, :], in_=hat_rows[0:8, :])
        nc.vector.memset(hat_sb[32:64, :], 0.0)
        nc.vector.memset(hat_sb[64:128, :], 0.0)
        b2_bf = const.tile([P, 4], BF16)
        nc.scalar.dma_start(out=b2_bf[:], in_=b2.rearrange("(i j) -> i j", j=4))

        warm_in = const.tile([P, 1], F32)
        warm_out = const.tile([P, 1], F32)
        nc.vector.memset(warm_in[:], 0.0)
        nc.scalar.activation(out=warm_out[:], in_=warm_in[:], func=ACT.Exp)

        ident = const.tile([P, P], F32)
        make_identity(nc, ident[:])

        w_sb = const.tile([P, 4, C], BF16)
        nc.sync.dma_start(out=w_sb[:], in_=w2.rearrange("(i j) c -> i j c", j=4))
        x_sb = []
        for b in range(B):
            row = []
            for k in range(3):
                xt = xin.tile([P, 4, C], BF16, name="x%d_%d" % (k, b), tag="x%d" % k)
                src = xs[k][b].rearrange("w h c -> (w h) c").rearrange("(p j) c -> p j c", j=4)
                nc.sync.dma_start(out=xt[:], in_=src)
                row.append(xt)
            x_sb.append(row)

        aux_ps = psum.tile([P, 2, P], F32, tag="o")
        hat_w = hat_sb[:].bitcast(F32)
        for u in range(2):
            nc.tensor.transpose(aux_ps[:, u, :], hat_w[:, P * u : P * u + P], ident[:])
        logit = const.tile([P, 16, 3, 2], F32)
        nc.vector.tensor_copy(
            out=logit[:].rearrange("q (u b) k e -> q u (b k e)", u=2),
            in_=aux_ps[:].bitcast(BF16)[:, :, 0:48],
        )
        top = const.tile([P, 16, 2], F32)
        nc.vector.tensor_reduce(
            out=top[:], in_=logit[:].rearrange("q a k e -> q a e k"), axis=AX.X, op=ALU.max
        )
        shifted = const.tile([P, 16, 3, 2], F32)
        nc.vector.tensor_tensor(
            out=shifted[:], in0=logit[:], in1=top[:].unsqueeze(2).to_broadcast([P, 16, 3, 2]),
            op=ALU.subtract,
        )
        expd = const.tile([P, 16, 3, 2], F32)
        nc.scalar.activation(out=expd[:], in_=shifted[:], func=ACT.Exp)
        total = const.tile([P, 16, 2], F32)
        nc.vector.tensor_reduce(
            out=total[:], in_=expd[:].rearrange("q a k e -> q a e k"), axis=AX.X, op=ALU.add
        )
        inv = const.tile([P, 16, 2], F32)
        nc.vector.reciprocal(out=inv[:], in_=total[:])
        gate = const.tile([P, 16, 3, 2], F32)
        nc.vector.tensor_tensor(
            out=gate[:], in0=expd[:], in1=inv[:].unsqueeze(2).to_broadcast([P, 16, 3, 2]),
            op=ALU.mult,
        )

        w_codes = const.tile([P, C], U32, align_bytes=64)
        w_scales = const.tile([P, C], U8, align_bytes=64)
        w_grouped = const.tile([P, 4 * C], BF16, align_bytes=64)
        w_words = w_sb[:].bitcast(F32)
        w_pairs = w_grouped[:].bitcast(F32).rearrange("q (c u) -> q c u", u=2)
        for h in range(2):
            w_ps = psum.tile([P, 2, 2, P], F32, tag="o")
            for u in range(2):
                for jj in range(2):
                    nc.tensor.transpose(
                        w_ps[:, u, jj, :], w_words[:, 2 * h + jj, P * u : P * u + P], ident[:]
                    )
            copy = nc.vector.tensor_copy if h == 0 else nc.scalar.copy
            copy(
                out=w_pairs[:, 256 * h : 256 * h + 256, :],
                in_=w_ps[:].rearrange("q u jj i -> q (jj i) u"),
            )
        b2_f = const.tile([P, 4], F32)
        nc.vector.tensor_copy(out=b2_f[:], in_=b2_bf[:])
        nc.vector.quantize_mx(out=w_codes[:].bitcast(FP8X4), scales=w_scales[:], in_=w_grouped[:])

        def half_view(bank, e):
            v = bank[:].bitcast(BF16).rearrange("q j (p e) -> q j p e", e=2)
            return v[:, :, :, e].rearrange("q j p -> q p j")

        banks = {}
        t0s = {}
        t1s = {}
        planes = {}
        grouped = {}
        codes = {}
        scales = {}
        o_sbs = {}

        def gate_of(n, k, e):
            return gate[:, 8 * (n % 2) + n // 2, k, e : e + 1]

        def transposes(n, k):
            if n >= UNITS:
                return
            b, u = n // 2, n % 2
            bank = psum.tile([P, 4, P], F32, name="bank%d" % k, tag="t%d" % k)
            xw = x_sb[b][k][:].bitcast(F32)
            for j in range(4):
                nc.tensor.transpose(bank[:, j, :], xw[:, j, P * u : P * u + P], ident[:])
            banks[(n, k)] = bank

        def pass1(n):
            if n >= UNITS:
                return
            for e in range(2):
                t0 = work.tile([P, P, 4], F32, name="t0", bufs=8)
                nc.scalar.activation(
                    out=t0[:], in_=half_view(banks[(n, 0)], e), func=ACT.Copy, scale=gate_of(n, 0, e)
                )
                t0s[(n, e)] = t0

        def pass2(n, e):
            t1 = work.tile([P, P, 4], F32, name="t1")
            nc.vector.scalar_tensor_tensor(
                out=t1[:], in0=half_view(banks[(n, 1)], e), scalar=gate_of(n, 1, e),
                in1=t0s[(n, e)][:], op0=ALU.mult, op1=ALU.add,
            )
            t1s[(n, e)] = t1

        def pass3(n):
            b, u = n // 2, n % 2
            if u == 0:
                planes[b] = stage.tile([P, 4, TOK], BF16, name="planes")
            for e in range(2):
                nc.vector.scalar_tensor_tensor(
                    out=planes[b][:, 2 * u + e, :].rearrange("q (p j) -> q p j", j=4),
                    in0=half_view(banks[(n, 2)], e), scalar=gate_of(n, 2, e),
                    in1=t1s[(n, e)][:], op0=ALU.mult, op1=ALU.add,
                )

        def regroup(b):
            grouped[b] = stage.tile([P, TOK, 4], BF16, name="grouped", align_bytes=64)
            nc.gpsimd.tensor_scalar(
                out=grouped[b][:], in0=planes[b][:].rearrange("q t n -> q n t"), scalar1=1.0,
                scalar2=0.0, op0=ALU.mult, op1=ALU.add,
            )

        def quantise(b, lo, hi):
            if lo == 0:
                codes[b] = stage.tile([P, TOK], U32, name="codes", align_bytes=64)
                scales[b] = stage.tile([P, TOK], U8, name="scales", align_bytes=64)
            nc.vector.quantize_mx(
                out=codes[b][:, lo:hi].bitcast(FP8X4), scales=scales[b][:, lo:hi],
                in_=grouped[b][:, lo:hi, :].rearrange("q n t -> q (n t)"),
            )

        def one_pass(b, j, lo, hi, tag):
            acc = psum.tile([P, hi - lo], F32, name="acc", tag=tag)
            nc.tensor.matmul_mx(
                out=acc[:],
                lhsT=w_codes[:, P * j : P * j + P].bitcast(FP8X4),
                lhsT_scale=w_scales[:, P * j : P * j + P],
                rhs=codes[b][:, lo:hi].bitcast(FP8X4),
                rhs_scale=scales[b][:, lo:hi],
                start=True,
                stop=True,
            )
            return acc

        def way_out(b, j, lo, hi, acc, on_vector):
            if on_vector:
                nc.vector.tensor_scalar_add(
                    out=o_sbs[b][:, j, lo:hi], in0=acc[:], scalar1=b2_f[:, j : j + 1]
                )
            else:
                nc.scalar.activation(
                    out=o_sbs[b][:, j, lo:hi], in_=acc[:], func=ACT.Identity,
                    bias=b2_f[:, j : j + 1], scale=1.0,
                )

        def store(b, j0, lo, hi, eng):
            dst = out[b].rearrange("(i j) w h -> i j (w h)", j=4)
            eng.dma_start(out=dst[:, j0 : j0 + 2, lo:hi], in_=o_sbs[b][:, j0 : j0 + 2, lo:hi])

        def project(b, j0, tag):
            if j0 == 0:
                o_sbs[b] = stage.tile([P, 4, TOK], F32, name="o_sb")
            for j in (j0, j0 + 1):
                way_out(b, j, 0, TOK, one_pass(b, j, 0, TOK, tag), False)
            store(b, j0, 0, TOK, nc.scalar)

        for n in range(2):
            for k in range(3):
                transposes(n, k)
            pass1(n)
        transposes(2, 0)
        pass1(2)
        for n in range(UNITS):
            transposes(n + 3, 0)
            pass1(n + 3)
            if n % 2 == 0 and n >= 4:
                project((n - 4) // 2, 2, "o")
            pass2(n, 0)
            if n == UNITS - 1:
                quantise(B - 2, 0, TOK)
                project(B - 2, 0, "o")
                project(B - 2, 2, "t0")
            pass2(n, 1)
            transposes(n + 2, 1)
            if n % 2 == 1 and 3 <= n < UNITS - 1:
                quantise((n - 3) // 2, 0, TOK)
                project((n - 3) // 2, 0, "o")
            pass3(n)
            transposes(n + 2, 2)
            if n % 2 == 1 and n < UNITS - 1:
                regroup(n // 2)

        b = B - 1
        HALF = TOK // 2
        g = stage.tile([P, TOK, 4], BF16, name="grouped", align_bytes=64)
        grouped[b] = g
        src = planes[b][:].rearrange("q t n -> q n t")
        nc.vector.tensor_copy(out=g[:, 0:HALF, :], in_=src[:, 0:HALF, :])
        nc.gpsimd.tensor_scalar(
            out=g[:, 384:TOK, :], in0=src[:, 384:TOK, :], scalar1=1.0, scalar2=0.0,
            op0=ALU.mult, op1=ALU.add,
        )
        nc.vector.tensor_copy(out=g[:, HALF:384, :], in_=src[:, HALF:384, :])
        quantise(b, 0, HALF)
        quantise(b, HALF, TOK)
        o_sbs[b] = stage.tile([P, 4, TOK], F32, name="o_sb")
        for h, tags in ((0, ("t1", "t1", "t2", "t2")), (1, ("o", "o", "t0", "t0"))):
            lo, hi = h * HALF, h * HALF + HALF
            accs = [one_pass(b, j, lo, hi, tags[j]) for j in range(4)]
            for j in range(4):
                way_out(b, j, lo, hi, accs[j], j % 2 == 1)
                if j % 2 == 1:
                    store(b, j - 1, lo, hi, nc.sync)
